import numpy as np
import ml_dtypes

BF16 = ml_dtypes.bfloat16


def bf(x):
    return np.asarray(x, np.float32).astype(BF16)


def f32(x):
    return np.asarray(x, np.float32)


def f64(x):
    return np.asarray(x).astype(np.float64)


def striped(idx):
    return np.tile(idx.reshape(-1, 16).T, (8, 1))


C, Bm, Dm, S, N = 384, 128, 3, 4096, 64
SIGMA2 = 1.0


def setup_inputs():
    return {"x": f32(np.random.standard_normal((C, S))), "offs": striped(np.random.permutation(S)[:N])}


def reference(x, offs):
    idx = offs[:16].T.reshape(-1)
    p = f64(x)[:, idx].reshape(Dm, Bm, N)
    diff = p[:, :, :, None] - p[:, :, None, :]
    d2 = (diff * diff).sum(axis=0)
    a = -np.exp(-np.sqrt(d2) / SIGMA2)
    rows = a.sum(axis=2)
    eye = np.arange(N)
    a[:, eye, eye] = -rows
    return a.reshape(Bm, N * N)

@@ -1,0 +1,69 @@
+import concourse.mybir as mybir
+
+F32 = mybir.dt.float32
+U16 = mybir.dt.uint16
+ACT = mybir.ActivationFunctionType
+ALU = mybir.AluOpType
+AXIS_X = mybir.AxisListType.X
+
+MOLECULES = 128
+COORDS = 3
+ATOMS = 4096
+PICKED = 64
+BLOCK_ROWS = 16
+BLOCKS = PICKED // BLOCK_ROWS
+BLOCK = BLOCK_ROWS * PICKED
+
+
+def tile_coords2stress_kernel(tc, x, offs, out):
+    nc = tc.nc
+    with tc.tile_pool(name="held", bufs=1) as held, tc.tile_pool(name="work", bufs=2) as work:
+        offsets = held.tile([MOLECULES, PICKED // 16], U16, name="offsets")
+        nc.sync.dma_start(offsets[:], offs)
+
+        tables = []
+        for d in range(COORDS):
+            table = held.tile([MOLECULES, ATOMS], F32, name=f"table{d}")
+            nc.sync.dma_start(table[:], x[d * MOLECULES : (d + 1) * MOLECULES, :])
+            tables.append(table)
+
+        dist2 = held.tile([MOLECULES, PICKED * PICKED], F32, name="dist2")
+        for d in range(COORDS):
+            picked = held.tile([MOLECULES, PICKED], F32, name=f"picked{d}")
+            nc.scalar.activation(picked[:], tables[d][:].indirect(offsets[:]), ACT.Copy)
+
+            for k in range(BLOCKS):
+                shape = [MOLECULES, BLOCK_ROWS, PICKED]
+                block = slice(k * BLOCK, (k + 1) * BLOCK)
+                at_j = picked[:].unsqueeze(1).to_broadcast(shape)
+                at_i = picked[:, k * BLOCK_ROWS : (k + 1) * BLOCK_ROWS].unsqueeze(2).to_broadcast(shape)
+                diff = work.tile(shape, F32, name="diff")
+                nc.vector.tensor_tensor(diff[:], at_j, at_i, ALU.subtract)
+                flat = diff[:].rearrange("b i j -> b (i j)")
+                if d == 0:
+                    nc.scalar.activation(dist2[:, block], flat, ACT.Square)
+                else:
+                    square = work.tile([MOLECULES, BLOCK], F32, name="square")
+                    nc.scalar.activation(square[:], flat, ACT.Square)
+                    nc.vector.tensor_tensor(dist2[:, block], dist2[:, block], square[:], ALU.add)
+
+        dist = held.tile([MOLECULES, PICKED * PICKED], F32, name="dist")
+        for k in range(BLOCKS):
+            block = slice(k * BLOCK, (k + 1) * BLOCK)
+            nc.scalar.activation(dist[:, block], dist2[:, block], ACT.Sqrt)
+
+        decay = held.tile([MOLECULES, PICKED * PICKED], F32, name="decay")
+        result = held.tile([MOLECULES, PICKED * (PICKED + 1)], F32, name="result")
+        diagonal = result[:].rearrange("b (i c) -> b i c", c=PICKED + 1)[:, :, 0]
+        for k in range(BLOCKS):
+            block = slice(k * BLOCK, (k + 1) * BLOCK)
+            rows = slice(k * BLOCK_ROWS, (k + 1) * BLOCK_ROWS)
+            nc.scalar.activation(decay[:, block], dist[:, block], ACT.Exp, scale=-1.0)
+            nc.vector.tensor_scalar_mul(result[:, block], decay[:, block], -1.0)
+            nc.vector.tensor_reduce(
+                diagonal[:, rows],
+                decay[:, block].rearrange("b (i j) -> b i j", j=PICKED),
+                AXIS_X,
+                ALU.add,
+            )
+            nc.sync.dma_start(out[:, block], result[:, block])

@@ -33,19 +33,22 @@ def tile_coords2stress_kernel(tc, x, offs, out):
             nc.scalar.activation(picked[:], tables[d][:].indirect(offsets[:]), ACT.Copy)
 
             for k in range(BLOCKS):
-                shape = [MOLECULES, BLOCK_ROWS, PICKED]
                 block = slice(k * BLOCK, (k + 1) * BLOCK)
-                at_j = picked[:].unsqueeze(1).to_broadcast(shape)
-                at_i = picked[:, k * BLOCK_ROWS : (k + 1) * BLOCK_ROWS].unsqueeze(2).to_broadcast(shape)
-                diff = work.tile(shape, F32, name="diff")
-                nc.vector.tensor_tensor(diff[:], at_j, at_i, ALU.subtract)
-                flat = diff[:].rearrange("b i j -> b (i j)")
                 if d == 0:
-                    nc.scalar.activation(dist2[:, block], flat, ACT.Square)
+                    square = dist2[:, block]
                 else:
-                    square = work.tile([MOLECULES, BLOCK], F32, name="square")
-                    nc.scalar.activation(square[:], flat, ACT.Square)
-                    nc.vector.tensor_tensor(dist2[:, block], dist2[:, block], square[:], ALU.add)
+                    square = work.tile([MOLECULES, BLOCK], F32, name="square")[:]
+                for r in range(BLOCK_ROWS):
+                    i = k * BLOCK_ROWS + r
+                    nc.scalar.activation(
+                        square[:, r * PICKED : (r + 1) * PICKED],
+                        picked[:],
+                        ACT.Square,
+                        bias=picked[:, i : i + 1],
+                        scale=-1.0,
+                    )
+                if d > 0:
+                    nc.vector.tensor_tensor(dist2[:, block], dist2[:, block], square, ALU.add)
 
         dist = held.tile([MOLECULES, PICKED * PICKED], F32, name="dist")
         for k in range(BLOCKS):

@@ -10,13 +10,13 @@ MOLECULES = 128
 COORDS = 3
 ATOMS = 4096
 PICKED = 64
-BLOCK_ROWS = 16
-BLOCKS = PICKED // BLOCK_ROWS
-BLOCK = BLOCK_ROWS * PICKED
+EDGE = 16
+BANDS = PICKED // EDGE
 
 
 def tile_coords2stress_kernel(tc, x, offs, out):
     nc = tc.nc
+    matrix_shape = [MOLECULES, PICKED, PICKED]
     with tc.tile_pool(name="held", bufs=1) as held, tc.tile_pool(name="work", bufs=2) as work:
         offsets = held.tile([MOLECULES, PICKED // 16], U16, name="offsets")
         nc.sync.dma_start(offsets[:], offs)
@@ -27,46 +27,55 @@ def tile_coords2stress_kernel(tc, x, offs, out):
             nc.sync.dma_start(table[:], x[d * MOLECULES : (d + 1) * MOLECULES, :])
             tables.append(table)
 
-        dist2 = held.tile([MOLECULES, PICKED * PICKED], F32, name="dist2")
+        rows = [slice(k * EDGE, (k + 1) * EDGE) for k in range(BANDS)]
+        right = [slice(k * EDGE, PICKED) for k in range(BANDS)]
+
+        dist2 = held.tile(matrix_shape, F32, name="dist2")
         for d in range(COORDS):
             picked = held.tile([MOLECULES, PICKED], F32, name=f"picked{d}")
             nc.scalar.activation(picked[:], tables[d][:].indirect(offsets[:]), ACT.Copy)
 
-            for k in range(BLOCKS):
-                block = slice(k * BLOCK, (k + 1) * BLOCK)
+            for k in range(BANDS):
                 if d == 0:
-                    square = dist2[:, block]
+                    square = dist2[:, rows[k], right[k]]
                 else:
-                    square = work.tile([MOLECULES, BLOCK], F32, name="square")[:]
-                for r in range(BLOCK_ROWS):
-                    i = k * BLOCK_ROWS + r
+                    square = work.tile([MOLECULES, EDGE, PICKED - k * EDGE], F32, name="square")[:]
+                for r in range(EDGE):
+                    i = k * EDGE + r
                     nc.scalar.activation(
-                        square[:, r * PICKED : (r + 1) * PICKED],
-                        picked[:],
+                        square[:, r, :],
+                        picked[:, right[k]],
                         ACT.Square,
                         bias=picked[:, i : i + 1],
                         scale=-1.0,
                     )
                 if d > 0:
-                    nc.vector.tensor_tensor(dist2[:, block], dist2[:, block], square, ALU.add)
+                    nc.vector.tensor_tensor(
+                        dist2[:, rows[k], right[k]], dist2[:, rows[k], right[k]], square, ALU.add
+                    )
 
-        dist = held.tile([MOLECULES, PICKED * PICKED], F32, name="dist")
-        for k in range(BLOCKS):
-            block = slice(k * BLOCK, (k + 1) * BLOCK)
-            nc.scalar.activation(dist[:, block], dist2[:, block], ACT.Sqrt)
+        dist = held.tile(matrix_shape, F32, name="dist")
+        for k in range(BANDS):
+            nc.scalar.activation(dist[:, rows[k], right[k]], dist2[:, rows[k], right[k]], ACT.Sqrt)
 
-        decay = held.tile([MOLECULES, PICKED * PICKED], F32, name="decay")
+        decay = held.tile(matrix_shape, F32, name="decay")
         result = held.tile([MOLECULES, PICKED * (PICKED + 1)], F32, name="result")
+        matrix = result[:, 0 : PICKED * PICKED].rearrange("b (i j) -> b i j", j=PICKED)
         diagonal = result[:].rearrange("b (i c) -> b i c", c=PICKED + 1)[:, :, 0]
-        for k in range(BLOCKS):
-            block = slice(k * BLOCK, (k + 1) * BLOCK)
-            rows = slice(k * BLOCK_ROWS, (k + 1) * BLOCK_ROWS)
-            nc.scalar.activation(decay[:, block], dist[:, block], ACT.Exp, scale=-1.0)
-            nc.vector.tensor_scalar_mul(result[:, block], decay[:, block], -1.0)
-            nc.vector.tensor_reduce(
-                diagonal[:, rows],
-                decay[:, block].rearrange("b (i j) -> b i j", j=PICKED),
-                AXIS_X,
-                ALU.add,
+        row_sums = held.tile([MOLECULES, PICKED], F32, name="row_sums")
+        for k in range(BANDS):
+            if k > 0:
+                left = slice(0, k * EDGE)
+                nc.scalar.mul(
+                    matrix[:, rows[k], left],
+                    decay[:, left, rows[k]].rearrange("b j i -> b i j"),
+                    -1.0,
+                )
+            nc.scalar.activation(
+                decay[:, rows[k], right[k]], dist[:, rows[k], right[k]], ACT.Exp, scale=-1.0
             )
-            nc.sync.dma_start(out[:, block], result[:, block])
+            nc.vector.tensor_scalar_mul(matrix[:, rows[k], right[k]], decay[:, rows[k], right[k]], -1.0)
+            nc.vector.tensor_reduce(row_sums[:, rows[k]], matrix[:, rows[k], :], AXIS_X, ALU.add)
+            nc.vector.tensor_scalar_mul(diagonal[:, rows[k]], row_sums[:, rows[k]], -1.0)
+            band = slice(k * EDGE * PICKED, (k + 1) * EDGE * PICKED)
+            nc.sync.dma_start(out[:, band], result[:, band])

@@ -12,6 +12,7 @@ ATOMS = 4096
 PICKED = 64
 EDGE = 16
 BANDS = PICKED // EDGE
+VECTOR_BANDS = range(BANDS // 2, BANDS)
 
 
 def tile_coords2stress_kernel(tc, x, offs, out):
@@ -30,52 +31,75 @@ def tile_coords2stress_kernel(tc, x, offs, out):
         rows = [slice(k * EDGE, (k + 1) * EDGE) for k in range(BANDS)]
         right = [slice(k * EDGE, PICKED) for k in range(BANDS)]
 
+        warm = held.tile([MOLECULES, 1], F32, name="warm")
+        nc.vector.memset(warm[:], 1.0)
+        nc.scalar.activation(warm[:], warm[:], ACT.Sqrt)
+
         dist2 = held.tile(matrix_shape, F32, name="dist2")
         for d in range(COORDS):
             picked = held.tile([MOLECULES, PICKED], F32, name=f"picked{d}")
             nc.scalar.activation(picked[:], tables[d][:].indirect(offsets[:]), ACT.Copy)
 
-            for k in range(BANDS):
-                if d == 0:
-                    square = dist2[:, rows[k], right[k]]
-                else:
-                    square = work.tile([MOLECULES, EDGE, PICKED - k * EDGE], F32, name="square")[:]
-                for r in range(EDGE):
-                    i = k * EDGE + r
-                    nc.scalar.activation(
-                        square[:, r, :],
-                        picked[:, right[k]],
-                        ACT.Square,
-                        bias=picked[:, i : i + 1],
-                        scale=-1.0,
+            squares = dist2 if d == 0 else work.tile(matrix_shape, F32, name="squares")
+            diffs = work.tile(matrix_shape, F32, name="diffs")
+            for k in reversed(range(BANDS)):
+                band_shape = [MOLECULES, EDGE, PICKED - k * EDGE]
+                square = squares[:, rows[k], right[k]]
+                if k in VECTOR_BANDS:
+                    diff = diffs[:, rows[k], right[k]]
+                    nc.vector.tensor_tensor(
+                        diff,
+                        picked[:, right[k]].unsqueeze(1).to_broadcast(band_shape),
+                        picked[:, rows[k]].unsqueeze(2).to_broadcast(band_shape),
+                        ALU.subtract,
                     )
+                    nc.vector.tensor_tensor(square, diff, diff, ALU.mult)
+                else:
+                    for r in range(EDGE):
+                        i = k * EDGE + r
+                        nc.scalar.activation(
+                            square[:, r, :],
+                            picked[:, right[k]],
+                            ACT.Square,
+                            bias=picked[:, i : i + 1],
+                            scale=-1.0,
+                        )
                 if d > 0:
                     nc.vector.tensor_tensor(
                         dist2[:, rows[k], right[k]], dist2[:, rows[k], right[k]], square, ALU.add
                     )
 
         dist = held.tile(matrix_shape, F32, name="dist")
-        for k in range(BANDS):
+        for k in reversed(range(BANDS)):
             nc.scalar.activation(dist[:, rows[k], right[k]], dist2[:, rows[k], right[k]], ACT.Sqrt)
 
         decay = held.tile(matrix_shape, F32, name="decay")
         result = held.tile([MOLECULES, PICKED * (PICKED + 1)], F32, name="result")
         matrix = result[:, 0 : PICKED * PICKED].rearrange("b (i j) -> b i j", j=PICKED)
         diagonal = result[:].rearrange("b (i c) -> b i c", c=PICKED + 1)[:, :, 0]
-        row_sums = held.tile([MOLECULES, PICKED], F32, name="row_sums")
+        right_sums = held.tile([MOLECULES, PICKED], F32, name="right_sums")
+        left_sums = held.tile([MOLECULES, PICKED], F32, name="left_sums")
         for k in range(BANDS):
-            if k > 0:
-                left = slice(0, k * EDGE)
-                nc.scalar.mul(
-                    matrix[:, rows[k], left],
-                    decay[:, left, rows[k]].rearrange("b j i -> b i j"),
-                    -1.0,
-                )
             nc.scalar.activation(
                 decay[:, rows[k], right[k]], dist[:, rows[k], right[k]], ACT.Exp, scale=-1.0
             )
-            nc.vector.tensor_scalar_mul(matrix[:, rows[k], right[k]], decay[:, rows[k], right[k]], -1.0)
-            nc.vector.tensor_reduce(row_sums[:, rows[k]], matrix[:, rows[k], :], AXIS_X, ALU.add)
-            nc.vector.tensor_scalar_mul(diagonal[:, rows[k]], row_sums[:, rows[k]], -1.0)
+            nc.gpsimd.tensor_scalar(
+                matrix[:, rows[k], right[k]], decay[:, rows[k], right[k]], -1.0, 0.0, ALU.mult, ALU.add
+            )
+            nc.vector.tensor_reduce(right_sums[:, rows[k]], decay[:, rows[k], right[k]], AXIS_X, ALU.add)
+            if k == 0:
+                nc.vector.tensor_copy(diagonal[:, rows[k]], right_sums[:, rows[k]])
+            else:
+                below = slice(k * EDGE, PICKED)
+                nc.scalar.mul(
+                    matrix[:, below, rows[k - 1]],
+                    decay[:, rows[k - 1], below].rearrange("b j i -> b i j"),
+                    -1.0,
+                )
+                left = slice(0, k * EDGE)
+                nc.vector.tensor_reduce(left_sums[:, rows[k]], matrix[:, rows[k], left], AXIS_X, ALU.add)
+                nc.vector.tensor_tensor(
+                    diagonal[:, rows[k]], right_sums[:, rows[k]], left_sums[:, rows[k]], ALU.subtract
+                )
             band = slice(k * EDGE * PICKED, (k + 1) * EDGE * PICKED)
             nc.sync.dma_start(out[:, band], result[:, band])

@@ -77,8 +77,9 @@ def tile_coords2stress_kernel(tc, x, offs, out):
         result = held.tile([MOLECULES, PICKED * (PICKED + 1)], F32, name="result")
         matrix = result[:, 0 : PICKED * PICKED].rearrange("b (i j) -> b i j", j=PICKED)
         diagonal = result[:].rearrange("b (i c) -> b i c", c=PICKED + 1)[:, :, 0]
-        right_sums = held.tile([MOLECULES, PICKED], F32, name="right_sums")
-        left_sums = held.tile([MOLECULES, PICKED], F32, name="left_sums")
+        RIGHT, LEFT = 0, 1
+        sums = held.tile([MOLECULES, PICKED, 2], F32, name="sums")
+        nc.vector.memset(sums[:, rows[0], LEFT], 0.0)
         for k in range(BANDS):
             nc.scalar.activation(
                 decay[:, rows[k], right[k]], dist[:, rows[k], right[k]], ACT.Exp, scale=-1.0
@@ -86,10 +87,8 @@ def tile_coords2stress_kernel(tc, x, offs, out):
             nc.gpsimd.tensor_scalar(
                 matrix[:, rows[k], right[k]], decay[:, rows[k], right[k]], -1.0, 0.0, ALU.mult, ALU.add
             )
-            nc.vector.tensor_reduce(right_sums[:, rows[k]], decay[:, rows[k], right[k]], AXIS_X, ALU.add)
-            if k == 0:
-                nc.vector.tensor_copy(diagonal[:, rows[k]], right_sums[:, rows[k]])
-            else:
+            nc.vector.tensor_reduce(sums[:, rows[k], RIGHT], decay[:, rows[k], right[k]], AXIS_X, ALU.add)
+            if k > 0:
                 below = slice(k * EDGE, PICKED)
                 nc.scalar.mul(
                     matrix[:, below, rows[k - 1]],
@@ -97,9 +96,9 @@ def tile_coords2stress_kernel(tc, x, offs, out):
                     -1.0,
                 )
                 left = slice(0, k * EDGE)
-                nc.vector.tensor_reduce(left_sums[:, rows[k]], matrix[:, rows[k], left], AXIS_X, ALU.add)
-                nc.vector.tensor_tensor(
-                    diagonal[:, rows[k]], right_sums[:, rows[k]], left_sums[:, rows[k]], ALU.subtract
+                nc.vector.tensor_reduce(
+                    sums[:, rows[k], LEFT], matrix[:, rows[k], left], AXIS_X, ALU.add, negate=True
                 )
+            nc.vector.tensor_reduce(diagonal[:, rows[k]], sums[:, rows[k], :], AXIS_X, ALU.add)
             band = slice(k * EDGE * PICKED, (k + 1) * EDGE * PICKED)
             nc.sync.dma_start(out[:, band], result[:, band])

@@ -77,9 +77,8 @@ def tile_coords2stress_kernel(tc, x, offs, out):
         result = held.tile([MOLECULES, PICKED * (PICKED + 1)], F32, name="result")
         matrix = result[:, 0 : PICKED * PICKED].rearrange("b (i j) -> b i j", j=PICKED)
         diagonal = result[:].rearrange("b (i c) -> b i c", c=PICKED + 1)[:, :, 0]
-        RIGHT, LEFT = 0, 1
-        sums = held.tile([MOLECULES, PICKED, 2], F32, name="sums")
-        nc.vector.memset(sums[:, rows[0], LEFT], 0.0)
+        right_sums = held.tile([MOLECULES, PICKED], F32, name="right_sums")
+        left_sums = held.tile([MOLECULES, PICKED], F32, name="left_sums")
         for k in range(BANDS):
             nc.scalar.activation(
                 decay[:, rows[k], right[k]], dist[:, rows[k], right[k]], ACT.Exp, scale=-1.0
@@ -87,18 +86,20 @@ def tile_coords2stress_kernel(tc, x, offs, out):
             nc.gpsimd.tensor_scalar(
                 matrix[:, rows[k], right[k]], decay[:, rows[k], right[k]], -1.0, 0.0, ALU.mult, ALU.add
             )
-            nc.vector.tensor_reduce(sums[:, rows[k], RIGHT], decay[:, rows[k], right[k]], AXIS_X, ALU.add)
-            if k > 0:
+            nc.vector.tensor_reduce(right_sums[:, rows[k]], decay[:, rows[k], right[k]], AXIS_X, ALU.add)
+            if k == 0:
+                nc.vector.tensor_copy(diagonal[:, rows[k]], right_sums[:, rows[k]])
+            else:
                 below = slice(k * EDGE, PICKED)
                 nc.scalar.mul(
-                    matrix[:, below, rows[k - 1]],
-                    decay[:, rows[k - 1], below].rearrange("b j i -> b i j"),
+                    matrix[:, below, rows[k - 1]].rearrange("b (q t) j -> b q j t", t=4),
+                    decay[:, rows[k - 1], below].rearrange("b j (q t) -> b q j t", t=4),
                     -1.0,
                 )
                 left = slice(0, k * EDGE)
-                nc.vector.tensor_reduce(
-                    sums[:, rows[k], LEFT], matrix[:, rows[k], left], AXIS_X, ALU.add, negate=True
+                nc.vector.tensor_reduce(left_sums[:, rows[k]], matrix[:, rows[k], left], AXIS_X, ALU.add)
+                nc.vector.tensor_tensor(
+                    diagonal[:, rows[k]], right_sums[:, rows[k]], left_sums[:, rows[k]], ALU.subtract
                 )
-            nc.vector.tensor_reduce(diagonal[:, rows[k]], sums[:, rows[k], :], AXIS_X, ALU.add)
             band = slice(k * EDGE * PICKED, (k + 1) * EDGE * PICKED)
             nc.sync.dma_start(out[:, band], result[:, band])

@@ -13,6 +13,7 @@ PICKED = 64
 EDGE = 16
 BANDS = PICKED // EDGE
 VECTOR_BANDS = range(BANDS // 2, BANDS)
+KEPT = 4
 
 
 def tile_coords2stress_kernel(tc, x, offs, out):
@@ -70,8 +71,11 @@ def tile_coords2stress_kernel(tc, x, offs, out):
                     )
 
         dist = held.tile(matrix_shape, F32, name="dist")
+        kept = slice(PICKED - KEPT, PICKED)
         for k in reversed(range(BANDS)):
-            nc.scalar.activation(dist[:, rows[k], right[k]], dist2[:, rows[k], right[k]], ACT.Sqrt)
+            early = slice(k * EDGE, PICKED - KEPT)
+            nc.scalar.activation(dist[:, rows[k], early], dist2[:, rows[k], early], ACT.Sqrt)
+        nc.scalar.activation(dist[:, :, kept], dist2[:, :, kept], ACT.Sqrt)
 
         decay = held.tile(matrix_shape, F32, name="decay")
         result = held.tile([MOLECULES, PICKED * (PICKED + 1)], F32, name="result")

@@ -43,7 +43,7 @@ def tile_coords2stress_kernel(tc, x, offs, out):
 
             squares = dist2 if d == 0 else work.tile(matrix_shape, F32, name="squares")
             diffs = work.tile(matrix_shape, F32, name="diffs")
-            for k in reversed(range(BANDS)):
+            for k in range(BANDS):
                 band_shape = [MOLECULES, EDGE, PICKED - k * EDGE]
                 square = squares[:, rows[k], right[k]]
                 if k in VECTOR_BANDS:
@@ -72,7 +72,7 @@ def tile_coords2stress_kernel(tc, x, offs, out):
 
         dist = held.tile(matrix_shape, F32, name="dist")
         kept = slice(PICKED - KEPT, PICKED)
-        for k in reversed(range(BANDS)):
+        for k in range(BANDS):
             early = slice(k * EDGE, PICKED - KEPT)
             nc.scalar.activation(dist[:, rows[k], early], dist2[:, rows[k], early], ACT.Sqrt)
         nc.scalar.activation(dist[:, :, kept], dist2[:, :, kept], ACT.Sqrt)
@@ -81,8 +81,8 @@ def tile_coords2stress_kernel(tc, x, offs, out):
         result = held.tile([MOLECULES, PICKED * (PICKED + 1)], F32, name="result")
         matrix = result[:, 0 : PICKED * PICKED].rearrange("b (i j) -> b i j", j=PICKED)
         diagonal = result[:].rearrange("b (i c) -> b i c", c=PICKED + 1)[:, :, 0]
-        right_sums = held.tile([MOLECULES, PICKED], F32, name="right_sums")
-        left_sums = held.tile([MOLECULES, PICKED], F32, name="left_sums")
+        sums = held.tile([MOLECULES, PICKED, 2], F32, name="sums")
+        nc.vector.memset(sums[:], 0.0)
         for k in range(BANDS):
             nc.scalar.activation(
                 decay[:, rows[k], right[k]], dist[:, rows[k], right[k]], ACT.Exp, scale=-1.0
@@ -90,10 +90,8 @@ def tile_coords2stress_kernel(tc, x, offs, out):
             nc.gpsimd.tensor_scalar(
                 matrix[:, rows[k], right[k]], decay[:, rows[k], right[k]], -1.0, 0.0, ALU.mult, ALU.add
             )
-            nc.vector.tensor_reduce(right_sums[:, rows[k]], decay[:, rows[k], right[k]], AXIS_X, ALU.add)
-            if k == 0:
-                nc.vector.tensor_copy(diagonal[:, rows[k]], right_sums[:, rows[k]])
-            else:
+            nc.vector.tensor_reduce(sums[:, rows[k], 0], decay[:, rows[k], right[k]], AXIS_X, ALU.add)
+            if k > 0:
                 below = slice(k * EDGE, PICKED)
                 nc.scalar.mul(
                     matrix[:, below, rows[k - 1]].rearrange("b (q t) j -> b q j t", t=4),
@@ -101,9 +99,9 @@ def tile_coords2stress_kernel(tc, x, offs, out):
                     -1.0,
                 )
                 left = slice(0, k * EDGE)
-                nc.vector.tensor_reduce(left_sums[:, rows[k]], matrix[:, rows[k], left], AXIS_X, ALU.add)
-                nc.vector.tensor_tensor(
-                    diagonal[:, rows[k]], right_sums[:, rows[k]], left_sums[:, rows[k]], ALU.subtract
+                nc.vector.tensor_reduce(
+                    sums[:, rows[k], 1], matrix[:, rows[k], left], AXIS_X, ALU.add, negate=True
                 )
+            nc.vector.tensor_reduce(diagonal[:, rows[k]], sums[:, rows[k], :], AXIS_X, ALU.add)
             band = slice(k * EDGE * PICKED, (k + 1) * EDGE * PICKED)
             nc.sync.dma_start(out[:, band], result[:, band])

@@ -21,13 +21,13 @@ def tile_coords2stress_kernel(tc, x, offs, out):
     matrix_shape = [MOLECULES, PICKED, PICKED]
     with tc.tile_pool(name="held", bufs=1) as held, tc.tile_pool(name="work", bufs=2) as work:
         offsets = held.tile([MOLECULES, PICKED // 16], U16, name="offsets")
-        nc.sync.dma_start(offsets[:], offs)
-
         tables = []
         for d in range(COORDS):
             table = held.tile([MOLECULES, ATOMS], F32, name=f"table{d}")
             nc.sync.dma_start(table[:], x[d * MOLECULES : (d + 1) * MOLECULES, :])
             tables.append(table)
+            if d == 0:
+                nc.sync.dma_start(offsets[:], offs)
 
         rows = [slice(k * EDGE, (k + 1) * EDGE) for k in range(BANDS)]
         right = [slice(k * EDGE, PICKED) for k in range(BANDS)]
@@ -84,13 +84,16 @@ def tile_coords2stress_kernel(tc, x, offs, out):
         sums = held.tile([MOLECULES, PICKED, 2], F32, name="sums")
         nc.vector.memset(sums[:], 0.0)
         for k in range(BANDS):
-            nc.scalar.activation(
-                decay[:, rows[k], right[k]], dist[:, rows[k], right[k]], ACT.Exp, scale=-1.0
-            )
+            height = EDGE // 2 if k == 0 else EDGE
+            for top in range(k * EDGE, (k + 1) * EDGE, height):
+                part = slice(top, top + height)
+                nc.scalar.activation(
+                    decay[:, part, right[k]], dist[:, part, right[k]], ACT.Exp, scale=-1.0
+                )
+                nc.vector.tensor_reduce(sums[:, part, 0], decay[:, part, right[k]], AXIS_X, ALU.add)
             nc.gpsimd.tensor_scalar(
                 matrix[:, rows[k], right[k]], decay[:, rows[k], right[k]], -1.0, 0.0, ALU.mult, ALU.add
             )
-            nc.vector.tensor_reduce(sums[:, rows[k], 0], decay[:, rows[k], right[k]], AXIS_X, ALU.add)
             if k > 0:
                 below = slice(k * EDGE, PICKED)
                 nc.scalar.mul(

@@ -10,9 +10,11 @@ MOLECULES = 128
 COORDS = 3
 ATOMS = 4096
 PICKED = 64
+STRIP = 8
+STRIPS = PICKED // STRIP
 EDGE = 16
 BANDS = PICKED // EDGE
-VECTOR_BANDS = range(BANDS // 2, BANDS)
+VECTOR_STRIPS = range(STRIPS // 2, STRIPS)
 KEPT = 4
 
 
@@ -29,6 +31,8 @@ def tile_coords2stress_kernel(tc, x, offs, out):
             if d == 0:
                 nc.sync.dma_start(offsets[:], offs)
 
+        strip_rows = [slice(s * STRIP, (s + 1) * STRIP) for s in range(STRIPS)]
+        strip_right = [slice(s * STRIP, PICKED) for s in range(STRIPS)]
         rows = [slice(k * EDGE, (k + 1) * EDGE) for k in range(BANDS)]
         right = [slice(k * EDGE, PICKED) for k in range(BANDS)]
 
@@ -43,39 +47,45 @@ def tile_coords2stress_kernel(tc, x, offs, out):
 
             squares = dist2 if d == 0 else work.tile(matrix_shape, F32, name="squares")
             diffs = work.tile(matrix_shape, F32, name="diffs")
-            for k in range(BANDS):
-                band_shape = [MOLECULES, EDGE, PICKED - k * EDGE]
-                square = squares[:, rows[k], right[k]]
-                if k in VECTOR_BANDS:
-                    diff = diffs[:, rows[k], right[k]]
+            for s in range(STRIPS):
+                strip_shape = [MOLECULES, STRIP, PICKED - s * STRIP]
+                square = squares[:, strip_rows[s], strip_right[s]]
+                if s in VECTOR_STRIPS:
+                    diff = diffs[:, strip_rows[s], strip_right[s]]
                     nc.vector.tensor_tensor(
                         diff,
-                        picked[:, right[k]].unsqueeze(1).to_broadcast(band_shape),
-                        picked[:, rows[k]].unsqueeze(2).to_broadcast(band_shape),
+                        picked[:, strip_right[s]].unsqueeze(1).to_broadcast(strip_shape),
+                        picked[:, strip_rows[s]].unsqueeze(2).to_broadcast(strip_shape),
                         ALU.subtract,
                     )
                     nc.vector.tensor_tensor(square, diff, diff, ALU.mult)
                 else:
-                    for r in range(EDGE):
-                        i = k * EDGE + r
+                    for r in range(STRIP):
+                        i = s * STRIP + r
                         nc.scalar.activation(
                             square[:, r, :],
-                            picked[:, right[k]],
+                            picked[:, strip_right[s]],
                             ACT.Square,
                             bias=picked[:, i : i + 1],
                             scale=-1.0,
                         )
                 if d > 0:
-                    nc.vector.tensor_tensor(
-                        dist2[:, rows[k], right[k]], dist2[:, rows[k], right[k]], square, ALU.add
-                    )
+                    strip_dist2 = dist2[:, strip_rows[s], strip_right[s]]
+                    nc.vector.tensor_tensor(strip_dist2, strip_dist2, square, ALU.add)
 
         dist = held.tile(matrix_shape, F32, name="dist")
         kept = slice(PICKED - KEPT, PICKED)
-        for k in range(BANDS):
-            early = slice(k * EDGE, PICKED - KEPT)
-            nc.scalar.activation(dist[:, rows[k], early], dist2[:, rows[k], early], ACT.Sqrt)
+        for s in range(STRIPS):
+            early = slice(s * STRIP, PICKED - KEPT)
+            nc.scalar.activation(dist[:, strip_rows[s], early], dist2[:, strip_rows[s], early], ACT.Sqrt)
         nc.scalar.activation(dist[:, :, kept], dist2[:, :, kept], ACT.Sqrt)
+
+        for k in range(BANDS):
+            upper, lower = strip_rows[2 * k], strip_rows[2 * k + 1]
+            nc.vector.tensor_copy(
+                dist[:, lower, upper].rearrange("b (q t) j -> b q j t", t=4),
+                dist[:, upper, lower].rearrange("b j (q t) -> b q j t", t=4),
+            )
 
         decay = held.tile(matrix_shape, F32, name="decay")
         result = held.tile([MOLECULES, PICKED * (PICKED + 1)], F32, name="result")

@@ -10,11 +10,12 @@ MOLECULES = 128
 COORDS = 3
 ATOMS = 4096
 PICKED = 64
+HALF = PICKED // 2
 STRIP = 8
-STRIPS = PICKED // STRIP
-EDGE = 16
-BANDS = PICKED // EDGE
-VECTOR_STRIPS = range(STRIPS // 2, STRIPS)
+SCALAR_STRIPS = [slice(top, top + STRIP) for top in range(0, HALF, STRIP)]
+LAST_STRIP = slice(PICKED - 2 * STRIP, PICKED)
+VECTOR_STRIPS = [slice(top, top + STRIP) for top in range(HALF, LAST_STRIP.start, STRIP)] + [LAST_STRIP]
+STRIPS = SCALAR_STRIPS + VECTOR_STRIPS
 KEPT = 4
 
 
@@ -31,11 +32,6 @@ def tile_coords2stress_kernel(tc, x, offs, out):
             if d == 0:
                 nc.sync.dma_start(offsets[:], offs)
 
-        strip_rows = [slice(s * STRIP, (s + 1) * STRIP) for s in range(STRIPS)]
-        strip_right = [slice(s * STRIP, PICKED) for s in range(STRIPS)]
-        rows = [slice(k * EDGE, (k + 1) * EDGE) for k in range(BANDS)]
-        right = [slice(k * EDGE, PICKED) for k in range(BANDS)]
-
         warm = held.tile([MOLECULES, 1], F32, name="warm")
         nc.vector.memset(warm[:], 1.0)
         nc.scalar.activation(warm[:], warm[:], ACT.Sqrt)
@@ -47,74 +43,86 @@ def tile_coords2stress_kernel(tc, x, offs, out):
 
             squares = dist2 if d == 0 else work.tile(matrix_shape, F32, name="squares")
             diffs = work.tile(matrix_shape, F32, name="diffs")
-            for s in range(STRIPS):
-                strip_shape = [MOLECULES, STRIP, PICKED - s * STRIP]
-                square = squares[:, strip_rows[s], strip_right[s]]
-                if s in VECTOR_STRIPS:
-                    diff = diffs[:, strip_rows[s], strip_right[s]]
-                    nc.vector.tensor_tensor(
-                        diff,
-                        picked[:, strip_right[s]].unsqueeze(1).to_broadcast(strip_shape),
-                        picked[:, strip_rows[s]].unsqueeze(2).to_broadcast(strip_shape),
-                        ALU.subtract,
-                    )
-                    nc.vector.tensor_tensor(square, diff, diff, ALU.mult)
-                else:
+            for strip in STRIPS:
+                right = slice(strip.start, PICKED)
+                square = squares[:, strip, right]
+                if strip in SCALAR_STRIPS:
                     for r in range(STRIP):
-                        i = s * STRIP + r
+                        i = strip.start + r
                         nc.scalar.activation(
                             square[:, r, :],
-                            picked[:, strip_right[s]],
+                            picked[:, right],
                             ACT.Square,
                             bias=picked[:, i : i + 1],
                             scale=-1.0,
                         )
+                else:
+                    strip_shape = [MOLECULES, strip.stop - strip.start, PICKED - strip.start]
+                    diff = diffs[:, strip, right]
+                    nc.vector.tensor_tensor(
+                        diff,
+                        picked[:, right].unsqueeze(1).to_broadcast(strip_shape),
+                        picked[:, strip].unsqueeze(2).to_broadcast(strip_shape),
+                        ALU.subtract,
+                    )
+                    if d < COORDS - 1:
+                        nc.scalar.activation(square, diff, ACT.Square)
+                    else:
+                        nc.vector.tensor_tensor(square, diff, diff, ALU.mult)
                 if d > 0:
-                    strip_dist2 = dist2[:, strip_rows[s], strip_right[s]]
+                    strip_dist2 = dist2[:, strip, right]
                     nc.vector.tensor_tensor(strip_dist2, strip_dist2, square, ALU.add)
 
         dist = held.tile(matrix_shape, F32, name="dist")
         kept = slice(PICKED - KEPT, PICKED)
-        for s in range(STRIPS):
-            early = slice(s * STRIP, PICKED - KEPT)
-            nc.scalar.activation(dist[:, strip_rows[s], early], dist2[:, strip_rows[s], early], ACT.Sqrt)
+        for strip in STRIPS:
+            early = slice(strip.start, PICKED - KEPT)
+            nc.scalar.activation(dist[:, strip, early], dist2[:, strip, early], ACT.Sqrt)
         nc.scalar.activation(dist[:, :, kept], dist2[:, :, kept], ACT.Sqrt)
 
-        for k in range(BANDS):
-            upper, lower = strip_rows[2 * k], strip_rows[2 * k + 1]
+        def mirror_dist(block_rows, block_columns):
             nc.vector.tensor_copy(
-                dist[:, lower, upper].rearrange("b (q t) j -> b q j t", t=4),
-                dist[:, upper, lower].rearrange("b j (q t) -> b q j t", t=4),
+                dist[:, block_rows, block_columns].rearrange("b (q t) j -> b q j t", t=4),
+                dist[:, block_columns, block_rows].rearrange("b j (q t) -> b q j t", t=4),
             )
+
+        for top in range(0, LAST_STRIP.start, 2 * STRIP):
+            mirror_dist(slice(top + STRIP, top + 2 * STRIP), slice(top, top + STRIP))
+        for top in range(0, PICKED, HALF):
+            mirror_dist(slice(top + HALF // 2, top + HALF), slice(top, top + HALF // 2))
 
         decay = held.tile(matrix_shape, F32, name="decay")
         result = held.tile([MOLECULES, PICKED * (PICKED + 1)], F32, name="result")
         matrix = result[:, 0 : PICKED * PICKED].rearrange("b (i j) -> b i j", j=PICKED)
         diagonal = result[:].rearrange("b (i c) -> b i c", c=PICKED + 1)[:, :, 0]
         sums = held.tile([MOLECULES, PICKED, 2], F32, name="sums")
-        nc.vector.memset(sums[:], 0.0)
-        for k in range(BANDS):
-            height = EDGE // 2 if k == 0 else EDGE
-            for top in range(k * EDGE, (k + 1) * EDGE, height):
-                part = slice(top, top + height)
-                nc.scalar.activation(
-                    decay[:, part, right[k]], dist[:, part, right[k]], ACT.Exp, scale=-1.0
-                )
-                nc.vector.tensor_reduce(sums[:, part, 0], decay[:, part, right[k]], AXIS_X, ALU.add)
-            nc.gpsimd.tensor_scalar(
-                matrix[:, rows[k], right[k]], decay[:, rows[k], right[k]], -1.0, 0.0, ALU.mult, ALU.add
+        def finish(top):
+            part = slice(top, top + STRIP)
+            partial_sums = 1 if top < HALF else 2
+            nc.vector.tensor_reduce(
+                diagonal[:, part], sums[:, part, 0:partial_sums], AXIS_X, ALU.add
             )
-            if k > 0:
-                below = slice(k * EDGE, PICKED)
+            store = slice(top * PICKED, (top + STRIP) * PICKED)
+            nc.sync.dma_start(out[:, store], result[:, store])
+
+        for top in range(0, PICKED, STRIP):
+            part = slice(top, top + STRIP)
+            right = slice(0 if top < HALF else HALF, PICKED)
+            nc.scalar.activation(decay[:, part, right], dist[:, part, right], ACT.Exp, scale=-1.0)
+            nc.vector.tensor_reduce(sums[:, part, 0], decay[:, part, right], AXIS_X, ALU.add)
+            nc.gpsimd.tensor_scalar(
+                matrix[:, part, right], decay[:, part, right], -1.0, 0.0, ALU.mult, ALU.add
+            )
+            if top >= HALF:
+                left = slice(0, HALF)
                 nc.scalar.mul(
-                    matrix[:, below, rows[k - 1]].rearrange("b (q t) j -> b q j t", t=4),
-                    decay[:, rows[k - 1], below].rearrange("b j (q t) -> b q j t", t=4),
+                    matrix[:, part, left].rearrange("b (q t) j -> b q j t", t=4),
+                    decay[:, left, part].rearrange("b j (q t) -> b q j t", t=4),
                     -1.0,
                 )
-                left = slice(0, k * EDGE)
                 nc.vector.tensor_reduce(
-                    sums[:, rows[k], 1], matrix[:, rows[k], left], AXIS_X, ALU.add, negate=True
+                    sums[:, part, 1], matrix[:, part, left], AXIS_X, ALU.add, negate=True
                 )
-            nc.vector.tensor_reduce(diagonal[:, rows[k]], sums[:, rows[k], :], AXIS_X, ALU.add)
-            band = slice(k * EDGE * PICKED, (k + 1) * EDGE * PICKED)
-            nc.sync.dma_start(out[:, band], result[:, band])
+            if top > 0:
+                finish(top - STRIP)
+        finish(PICKED - STRIP)

@@ -13,9 +13,11 @@ PICKED = 64
 HALF = PICKED // 2
 STRIP = 8
 SCALAR_STRIPS = [slice(top, top + STRIP) for top in range(0, HALF, STRIP)]
-LAST_STRIP = slice(PICKED - 2 * STRIP, PICKED)
-VECTOR_STRIPS = [slice(top, top + STRIP) for top in range(HALF, LAST_STRIP.start, STRIP)] + [LAST_STRIP]
-STRIPS = SCALAR_STRIPS + VECTOR_STRIPS
+VECTOR_STRIPS = [
+    [slice(HALF, PICKED)],
+    [slice(HALF, HALF + 2 * STRIP), slice(HALF + 2 * STRIP, PICKED)],
+    [slice(HALF, HALF + STRIP), slice(HALF + STRIP, HALF + 2 * STRIP), slice(HALF + 2 * STRIP, PICKED)],
+]
 KEPT = 4
 
 
@@ -33,7 +35,7 @@ def tile_coords2stress_kernel(tc, x, offs, out):
                 nc.sync.dma_start(offsets[:], offs)
 
         warm = held.tile([MOLECULES, 1], F32, name="warm")
-        nc.vector.memset(warm[:], 1.0)
+        nc.gpsimd.memset(warm[:], 1.0)
         nc.scalar.activation(warm[:], warm[:], ACT.Sqrt)
 
         dist2 = held.tile(matrix_shape, F32, name="dist2")
@@ -43,7 +45,7 @@ def tile_coords2stress_kernel(tc, x, offs, out):
 
             squares = dist2 if d == 0 else work.tile(matrix_shape, F32, name="squares")
             diffs = work.tile(matrix_shape, F32, name="diffs")
-            for strip in STRIPS:
+            for strip in SCALAR_STRIPS + VECTOR_STRIPS[d]:
                 right = slice(strip.start, PICKED)
                 square = squares[:, strip, right]
                 if strip in SCALAR_STRIPS:
@@ -75,7 +77,7 @@ def tile_coords2stress_kernel(tc, x, offs, out):
 
         dist = held.tile(matrix_shape, F32, name="dist")
         kept = slice(PICKED - KEPT, PICKED)
-        for strip in STRIPS:
+        for strip in SCALAR_STRIPS + VECTOR_STRIPS[-1]:
             early = slice(strip.start, PICKED - KEPT)
             nc.scalar.activation(dist[:, strip, early], dist2[:, strip, early], ACT.Sqrt)
         nc.scalar.activation(dist[:, :, kept], dist2[:, :, kept], ACT.Sqrt)
@@ -86,7 +88,7 @@ def tile_coords2stress_kernel(tc, x, offs, out):
                 dist[:, block_columns, block_rows].rearrange("b j (q t) -> b q j t", t=4),
             )
 
-        for top in range(0, LAST_STRIP.start, 2 * STRIP):
+        for top in range(0, HALF + 2 * STRIP, 2 * STRIP):
             mirror_dist(slice(top + STRIP, top + 2 * STRIP), slice(top, top + STRIP))
         for top in range(0, PICKED, HALF):
             mirror_dist(slice(top + HALF // 2, top + HALF), slice(top, top + HALF // 2))

@@ -112,9 +112,13 @@ def tile_coords2stress_kernel(tc, x, offs, out):
             right = slice(0 if top < HALF else HALF, PICKED)
             nc.scalar.activation(decay[:, part, right], dist[:, part, right], ACT.Exp, scale=-1.0)
             nc.vector.tensor_reduce(sums[:, part, 0], decay[:, part, right], AXIS_X, ALU.add)
+            split = top + STRIP // 2 if part.stop == HALF else part.stop
             nc.gpsimd.tensor_scalar(
-                matrix[:, part, right], decay[:, part, right], -1.0, 0.0, ALU.mult, ALU.add
+                matrix[:, top:split, right], decay[:, top:split, right], -1.0, 0.0, ALU.mult, ALU.add
             )
+            if split < part.stop:
+                rest = slice(split, part.stop)
+                nc.scalar.mul(matrix[:, rest, right], decay[:, rest, right], -1.0)
             if top >= HALF:
                 left = slice(0, HALF)
                 nc.scalar.mul(

@@ -45,7 +45,11 @@ def tile_coords2stress_kernel(tc, x, offs, out):
 
             squares = dist2 if d == 0 else work.tile(matrix_shape, F32, name="squares")
             diffs = work.tile(matrix_shape, F32, name="diffs")
-            for strip in SCALAR_STRIPS + VECTOR_STRIPS[d]:
+            if d < COORDS - 1:
+                strips = VECTOR_STRIPS[d] + SCALAR_STRIPS
+            else:
+                strips = SCALAR_STRIPS + VECTOR_STRIPS[d]
+            for strip in strips:
                 right = slice(strip.start, PICKED)
                 square = squares[:, strip, right]
                 if strip in SCALAR_STRIPS:

import concourse.mybir as mybir

F32 = mybir.dt.float32
U16 = mybir.dt.uint16
ACT = mybir.ActivationFunctionType
ALU = mybir.AluOpType
AXIS_X = mybir.AxisListType.X

MOLECULES = 128
COORDS = 3
ATOMS = 4096
PICKED = 64
HALF = PICKED // 2
STRIP = 8
SCALAR_STRIPS = [slice(top, top + STRIP) for top in range(0, HALF, STRIP)]
VECTOR_STRIPS = [
    [slice(HALF, PICKED)],
    [slice(HALF, HALF + 2 * STRIP), slice(HALF + 2 * STRIP, PICKED)],
    [slice(HALF, HALF + STRIP), slice(HALF + STRIP, HALF + 2 * STRIP), slice(HALF + 2 * STRIP, PICKED)],
]
KEPT = 4


def tile_coords2stress_kernel(tc, x, offs, out):
    nc = tc.nc
    matrix_shape = [MOLECULES, PICKED, PICKED]
    with tc.tile_pool(name="held", bufs=1) as held, tc.tile_pool(name="work", bufs=2) as work:
        offsets = held.tile([MOLECULES, PICKED // 16], U16, name="offsets")
        tables = []
        for d in range(COORDS):
            table = held.tile([MOLECULES, ATOMS], F32, name=f"table{d}")
            nc.sync.dma_start(table[:], x[d * MOLECULES : (d + 1) * MOLECULES, :])
            tables.append(table)
            if d == 0:
                nc.sync.dma_start(offsets[:], offs)

        warm = held.tile([MOLECULES, 1], F32, name="warm")
        nc.gpsimd.memset(warm[:], 1.0)
        nc.scalar.activation(warm[:], warm[:], ACT.Sqrt)

        dist2 = held.tile(matrix_shape, F32, name="dist2")
        for d in range(COORDS):
            picked = held.tile([MOLECULES, PICKED], F32, name=f"picked{d}")
            nc.scalar.activation(picked[:], tables[d][:].indirect(offsets[:]), ACT.Copy)

            squares = dist2 if d == 0 else work.tile(matrix_shape, F32, name="squares")
            diffs = work.tile(matrix_shape, F32, name="diffs")
            if d < COORDS - 1:
                strips = VECTOR_STRIPS[d] + SCALAR_STRIPS
            else:
                strips = SCALAR_STRIPS + VECTOR_STRIPS[d]
            for strip in strips:
                right = slice(strip.start, PICKED)
                square = squares[:, strip, right]
                if strip in SCALAR_STRIPS:
                    for r in range(STRIP):
                        i = strip.start + r
                        nc.scalar.activation(
                            square[:, r, :],
                            picked[:, right],
                            ACT.Square,
                            bias=picked[:, i : i + 1],
                            scale=-1.0,
                        )
                else:
                    strip_shape = [MOLECULES, strip.stop - strip.start, PICKED - strip.start]
                    diff = diffs[:, strip, right]
                    nc.vector.tensor_tensor(
                        diff,
                        picked[:, right].unsqueeze(1).to_broadcast(strip_shape),
                        picked[:, strip].unsqueeze(2).to_broadcast(strip_shape),
                        ALU.subtract,
                    )
                    if d < COORDS - 1:
                        nc.scalar.activation(square, diff, ACT.Square)
                    else:
                        nc.vector.tensor_tensor(square, diff, diff, ALU.mult)
                if d > 0:
                    strip_dist2 = dist2[:, strip, right]
                    nc.vector.tensor_tensor(strip_dist2, strip_dist2, square, ALU.add)

        dist = held.tile(matrix_shape, F32, name="dist")
        kept = slice(PICKED - KEPT, PICKED)
        for strip in SCALAR_STRIPS + VECTOR_STRIPS[-1]:
            early = slice(strip.start, PICKED - KEPT)
            nc.scalar.activation(dist[:, strip, early], dist2[:, strip, early], ACT.Sqrt)
        nc.scalar.activation(dist[:, :, kept], dist2[:, :, kept], ACT.Sqrt)

        def mirror_dist(block_rows, block_columns):
            nc.vector.tensor_copy(
                dist[:, block_rows, block_columns].rearrange("b (q t) j -> b q j t", t=4),
                dist[:, block_columns, block_rows].rearrange("b j (q t) -> b q j t", t=4),
            )

        for top in range(0, HALF + 2 * STRIP, 2 * STRIP):
            mirror_dist(slice(top + STRIP, top + 2 * STRIP), slice(top, top + STRIP))
        for top in range(0, PICKED, HALF):
            mirror_dist(slice(top + HALF // 2, top + HALF), slice(top, top + HALF // 2))

        decay = held.tile(matrix_shape, F32, name="decay")
        result = held.tile([MOLECULES, PICKED * (PICKED + 1)], F32, name="result")
        matrix = result[:, 0 : PICKED * PICKED].rearrange("b (i j) -> b i j", j=PICKED)
        diagonal = result[:].rearrange("b (i c) -> b i c", c=PICKED + 1)[:, :, 0]
        sums = held.tile([MOLECULES, PICKED, 2], F32, name="sums")
        def finish(top):
            part = slice(top, top + STRIP)
            partial_sums = 1 if top < HALF else 2
            nc.vector.tensor_reduce(
                diagonal[:, part], sums[:, part, 0:partial_sums], AXIS_X, ALU.add
            )
            store = slice(top * PICKED, (top + STRIP) * PICKED)
            nc.sync.dma_start(out[:, store], result[:, store])

        for top in range(0, PICKED, STRIP):
            part = slice(top, top + STRIP)
            right = slice(0 if top < HALF else HALF, PICKED)
            nc.scalar.activation(decay[:, part, right], dist[:, part, right], ACT.Exp, scale=-1.0)
            nc.vector.tensor_reduce(sums[:, part, 0], decay[:, part, right], AXIS_X, ALU.add)
            split = top + STRIP // 2 if part.stop == HALF else part.stop
            nc.gpsimd.tensor_scalar(
                matrix[:, top:split, right], decay[:, top:split, right], -1.0, 0.0, ALU.mult, ALU.add
            )
            if split < part.stop:
                rest = slice(split, part.stop)
                nc.scalar.mul(matrix[:, rest, right], decay[:, rest, right], -1.0)
            if top >= HALF:
                left = slice(0, HALF)
                nc.scalar.mul(
                    matrix[:, part, left].rearrange("b (q t) j -> b q j t", t=4),
                    decay[:, left, part].rearrange("b j (q t) -> b q j t", t=4),
                    -1.0,
                )
                nc.vector.tensor_reduce(
                    sums[:, part, 1], matrix[:, part, left], AXIS_X, ALU.add, negate=True
                )
            if top > 0:
                finish(top - STRIP)
        finish(PICKED - STRIP)
